import numpy as np
import ml_dtypes


def mxq(x, axis, fmt="e4m3"):
    dtype, down = {"e4m3": (ml_dtypes.float8_e4m3fn, 7), "e5m2": (ml_dtypes.float8_e5m2, 14)}[fmt]
    v = np.moveaxis(np.asarray(x, np.float32).astype(ml_dtypes.bfloat16).astype(np.float64), axis, -1)
    blocks = v.reshape(v.shape[:-1] + (-1, 32))
    amax = np.abs(blocks).max(-1, keepdims=True)
    byte = np.maximum(np.where(amax > 0, np.frexp(amax)[1] - 1 + 127, 0) - down, 1)
    scale = np.exp2(byte - 127.0)
    codes = (blocks / scale).astype(np.float32).astype(dtype).astype(np.float64)
    return np.moveaxis((codes * scale).reshape(v.shape), -1, axis)


WIDE = False


def mx_kscale(k):
    if not WIDE:
        return np.ones(k)
    levels = np.array([10, -10, 5, -5, 0])
    if k % 512:
        return np.exp2(np.random.permutation(np.resize(levels, k // 32))).repeat(32)
    a = np.empty((k // 512, 16))
    for p in range(k // 512):
        a[p, :8] = np.random.permutation(np.resize(levels, 8))
        for g in range(8):
            far = levels[np.abs(levels - a[p, g]) >= 10]
            a[p, g + 8] = far[np.random.randint(len(far))]
    return np.exp2(a.ravel()).repeat(32)


BF16 = ml_dtypes.bfloat16


def bf(x):
    return np.asarray(x, np.float32).astype(BF16)


def f64(x):
    return np.asarray(x).astype(np.float64)


B, S, D, H, DH = 4, 2048, 512, 2, 64
ROPE_BASE = 10000.0


def rope_tables():
    inv_freq = 1.0 / ROPE_BASE ** (np.arange(0, DH, 2) / DH)
    freqs = np.arange(S)[:, None] * inv_freq[None, :]
    emb = np.concatenate([freqs, freqs], axis=-1)
    return np.cos(emb), np.sin(emb)


def rotate_half(t):
    t1, t2 = t[..., : DH // 2], t[..., DH // 2 :]
    return np.concatenate([-t2, t1], axis=-1)


def draw0():
    s = mx_kscale(D)
    c, sn = rope_tables()
    return {"x": bf(np.random.standard_normal((B, S, D)) * s),
            "Wq": bf(np.random.standard_normal((H * DH, D)) / np.sqrt(D) / s[None, :]),
            "Wk": bf(np.random.standard_normal((H * DH, D)) / np.sqrt(D) / s[None, :]),
            "rope_cos": bf(c), "rope_sin": bf(sn)}


def core(x, Wq, Wk, rope_cos, rope_sin):
    xq = mxq(f64(x), 2, "e4m3")
    cos = f64(rope_cos)[None, None]
    sin = f64(rope_sin)[None, None]

    def proj(W):
        y = xq @ mxq(f64(W), 1, "e4m3").T
        return y.reshape(B, S, H, DH).transpose(0, 2, 1, 3)

    q, k = proj(Wq), proj(Wk)
    q_rot = q * cos + rotate_half(q) * sin
    k_rot = k * cos + rotate_half(k) * sin
    return q_rot, k_rot


def e4m3fn_bytes(y):
    return np.clip(np.asarray(y, np.float64), -448.0, 448.0).astype(np.float32).astype(ml_dtypes.float8_e4m3fn).view(np.uint8)


def e4m3fn_values(b):
    return np.asarray(b, np.uint8).view(ml_dtypes.float8_e4m3fn).astype(np.float64)


def setup_inputs():
    d = draw0()
    x0 = np.asarray(d['x']).astype(np.float64)
    s = (np.max(np.abs(x0), axis=(0, 1), keepdims=True) / 448.0).astype(np.float32)
    out = {}
    for k, v in d.items():
        if k == 'x':
            out['x_bytes'] = e4m3fn_bytes(x0 / s.astype(np.float64))
            out['x_scale'] = s
        else:
            out[k] = v
    return out


def reference(x_bytes, x_scale, Wq, Wk, rope_cos, rope_sin):
    return core(e4m3fn_values(x_bytes) * x_scale.astype(np.float64), Wq, Wk, rope_cos, rope_sin)

@@ -1,0 +1,223 @@
+from contextlib import ExitStack
+
+import concourse.mybir as mybir
+from concourse.masks import make_identity
+
+F32 = mybir.dt.float32
+BF16 = mybir.dt.bfloat16
+U32 = mybir.dt.uint32
+I32 = mybir.dt.int32
+U8 = mybir.dt.uint8
+FP8 = mybir.dt.float8_e4m3fn
+FP8X4 = mybir.dt.float8_e4m3fn_x4
+MULT = mybir.AluOpType.mult
+ADD = mybir.AluOpType.add
+COPY = mybir.ActivationFunctionType.Copy
+
+B, S, D = 4, 2048, 512
+P = 128
+TPP = S // P
+QPB = TPP // 4
+NQ = B * QPB
+PATH = "VUUUUUUUUUUUUUUU"
+LC = 4
+RVB = 48
+RG = 64
+RP = 256 - RVB
+FLOPS = 2 * B * S * D * 256
+
+
+def tile_attention_pa_t_kernel(tc, x_bytes, x_scale, Wq, Wk, rope_cos, rope_sin, out_0, out_1):
+    nc = tc.nc
+    with ExitStack() as ctx:
+        keep = ctx.enter_context(tc.tile_pool(name="keep", bufs=1))
+        xin = ctx.enter_context(tc.tile_pool(name="xin", bufs=2 * NQ))
+        deep = ctx.enter_context(tc.tile_pool(name="deep", bufs=2 * LC + 2))
+        xgp = ctx.enter_context(tc.tile_pool(name="xgp", bufs=1))
+        work = ctx.enter_context(tc.tile_pool(name="work", bufs=3))
+        outp = ctx.enter_context(tc.tile_pool(name="outp", bufs=4))
+        ps_t = ctx.enter_context(tc.psum_pool(name="ps_t", bufs=4))
+        ps_y = ctx.enter_context(tc.psum_pool(name="ps_y", bufs=4))
+
+        xb = []
+        for j in range(2 * NQ):
+            t = xin.tile([P, 2 * D], U8, name="xbytes", tag="xbytes")
+            xb.append(t)
+
+        def load(j):
+            b, pj = divmod(j, 2 * QPB)
+            src = x_bytes[b].rearrange("(p i) k -> p (i k)", i=TPP)
+            nc.sync.dma_start(out=xb[j][:], in_=src[:, pj * 2 * D:(pj + 1) * 2 * D])
+
+        load(0)
+        load(1)
+        w_raw = keep.tile([P, 2, D], BF16, name="w_raw")
+        nc.scalar.dma_start(out=w_raw[:, 0, :], in_=Wq)
+        nc.scalar.dma_start(out=w_raw[:, 1, :], in_=Wk)
+        s4 = keep.tile([P, 2, 2], F32, name="s4")
+        nc.scalar.dma_start(out=s4[:].rearrange("p u e -> p (u e)"), in_=x_scale.rearrange("a b (p t) -> p (a b t)", t=4))
+        tab = keep.tile([P, TPP, 2, 64], BF16, name="tab")
+        nc.scalar.dma_start(out=tab[:, :, 0, :], in_=rope_cos.rearrange("(p i) f -> p i f", i=TPP))
+        nc.scalar.dma_start(out=tab[:, :, 1, :], in_=rope_sin.rearrange("(p i) f -> p i f", i=TPP))
+        for j in range(2, 2 * NQ):
+            load(j)
+
+        ident = keep.tile([P, P], F32, name="ident")
+        make_identity(nc, ident[:])
+        nc.gpsimd.tensor_scalar(out=tab[:, :, 1, 0:32], in0=tab[:, :, 1, 0:32], scalar1=-1.0, scalar2=0.0, op0=MULT, op1=ADD)
+
+        wc = keep.tile([P, 512], U32, name="wc", align_bytes=64)
+        ws = keep.tile([P, 512], U8, name="ws", align_bytes=64)
+        wg = keep.tile([P, 1024], BF16, name="wg", align_bytes=64)
+        nc.vector.memset(ws[:].bitcast(I32), 0)
+        wt = ps_t.tile([P, 2, 256], F32, name="xt", tag="xt")
+        for qk in range(2):
+            words = w_raw[:, qk, :].bitcast(F32)
+            for u in range(2):
+                nc.tensor.transpose(wt[:, u, qk * P:(qk + 1) * P], words[:, u:256:2], ident[:])
+        nc.vector.tensor_copy(out=wg[:].bitcast(F32).rearrange("p (n u) -> p n u", u=2), in_=wt[:].rearrange("p u n -> p n u"))
+        nc.vector.quantize_mx(out=wc[:, 0:256].bitcast(FP8X4), scales=ws[:, 0:256], in_=wg[:])
+        wcv = wc[:].bitcast(I32).rearrange("p (c g h j) -> p c g h j", c=2, g=4, h=2)
+        wsv = ws[:].rearrange("p (c g h j) -> p c g h j", c=2, g=4, h=2)
+        for h in range(2):
+            nc.vector.tensor_copy(out=wcv[:, 1, :, h, :], in_=wcv[:, 0, :, 1 - h, :])
+            nc.vector.tensor_copy(out=wsv[:, 1, :, h, :], in_=wsv[:, 0, :, 1 - h, :])
+
+        st = {}
+
+        def cast(q):
+            for a in range(2):
+                vb = deep.tile([P, 2 * D], BF16, name="vb")
+                nc.scalar.copy(out=vb[:], in_=xb[2 * q + a][:].bitcast(FP8))
+                st[("vb", q, a)] = vb
+
+        def trans(q):
+            for a in range(2):
+                vw = st[("vb", q, a)][:].bitcast(F32)
+                xt = ps_t.tile([P, 2, 256], F32, name="xt", tag="xt")
+                for tl in range(2):
+                    for u in range(2):
+                        nc.tensor.transpose(xt[:, u, tl * P:(tl + 1) * P], vw[:, tl * 256 + u:(tl + 1) * 256:2], ident[:])
+                st[("xt", q, a)] = xt
+
+        def leave_s(q):
+            if PATH[q] == "U":
+                xt = st[("xt", q, 1)]
+                pl = work.tile([P, 4, RP], BF16, name="pl")
+                st[("pl", q)] = pl
+                for u in range(2):
+                    for e in range(2):
+                        nc.scalar.activation(out=pl[:, 2 * u + e, :], in_=xt[:].bitcast(BF16)[:, u, 2 * RVB + e:512:2], func=COPY, scale=s4[:, u, e:e + 1])
+
+        def new_xg(q):
+            xg = xgp.tile([P, 4 * D], BF16, name="xg", align_bytes=64)
+            st[("xg", q)] = xg
+
+        def inter(q):
+            if PATH[q] == "U":
+                nc.gpsimd.tensor_scalar(
+                    out=st[("xg", q)][:, 2 * D + 4 * RVB:2 * D + 4 * (RVB + RG)].rearrange("p (r t) -> p r t", t=4),
+                    in0=st[("pl", q)][:, :, 0:RG].rearrange("p t r -> p r t"),
+                    scalar1=1.0,
+                    scalar2=0.0,
+                    op0=MULT,
+                    op1=ADD,
+                )
+
+        def inter_s(q):
+            if PATH[q] == "U":
+                nc.scalar.copy(
+                    out=st[("xg", q)][:, 2 * D + 4 * (RVB + RG):4 * D].rearrange("p (r t) -> p r t", t=4),
+                    in_=st[("pl", q)][:, :, RG:RP].rearrange("p t r -> p r t"),
+                )
+
+        def leave_v(q):
+            xg = st[("xg", q)]
+            for a, n in ((0, 256), (1, 256 if PATH[q] == "V" else RVB)):
+                xt = st[("xt", q, a)]
+                nc.vector.tensor_tensor(
+                    out=xg[:, a * 1024:a * 1024 + 4 * n].rearrange("p (r u e) -> p r u e", u=2, e=2),
+                    in0=xt[:].bitcast(BF16)[:, :, 0:2 * n].rearrange("p u (r e) -> p r u e", e=2),
+                    in1=s4[:].unsqueeze(1).to_broadcast([P, n, 2, 2]),
+                    op=MULT,
+                )
+
+        def quant(q):
+            xc = work.tile([P, 4 * P], U32, name="xc", align_bytes=64)
+            xs = work.tile([P, 4 * P], U8, name="xs", align_bytes=64)
+            nc.vector.quantize_mx(out=xc[:].bitcast(FP8X4), scales=xs[:], in_=st[("xg", q)][:])
+            st[("xc", q)] = xc
+            st[("xs", q)] = xs
+
+        def mx(q, tl):
+            y = ps_y.tile([P, 512], F32, name="y")
+            cols = slice(tl * P, (tl + 1) * P)
+            nc.tensor.matmul_mx(
+                out=y[:],
+                lhsT=st[("xc", q)][:, cols].bitcast(FP8X4),
+                lhsT_scale=st[("xs", q)][:, cols],
+                rhs=wc[:].bitcast(FP8X4),
+                rhs_scale=ws[:],
+                start=True,
+                stop=True,
+            )
+            st[("y", q, tl)] = y
+
+        def group(q, t0, t1):
+            prod = outp.tile([P, 2, 4, t1 - t0, 64], F32, name="prod")
+            st[("prod", q)] = (prod, t0)
+
+        def mult(q, tl):
+            i = (q % QPB) * 4 + tl
+            prod, t0 = st[("prod", q)]
+            nc.vector.tensor_tensor(
+                out=prod[:, :, :, tl - t0, :],
+                in0=st[("y", q, tl)][:].rearrange("p (c g f) -> p c g f", c=2, g=4),
+                in1=tab[:, i, :, :].unsqueeze(2).to_broadcast([P, 2, 4, 64]),
+                op=MULT,
+            )
+
+        def add_store(q, t0, t1, eng):
+            b, m = divmod(q, QPB)
+            prod, t00 = st[("prod", q)]
+            stage = outp.tile([P, 4, t1 - t0, 64], F32, name="stage")
+            eng.tensor_tensor(out=stage[:], in0=prod[:, 0, :, :, :], in1=prod[:, 1, :, :, :], op=ADD)
+            for o, dst in enumerate((out_0, out_1)):
+                nc.sync.dma_start(
+                    out=dst[b].rearrange("h (p i) f -> p h (i f)", i=TPP)[:, :, (m * 4 + t0) * 64:(m * 4 + t1) * 64],
+                    in_=stage[:, 2 * o:2 * o + 2, :, :].rearrange("p g t f -> p g (t f)"),
+                )
+
+        def ok(q):
+            return 0 <= q < NQ
+
+        with tc.manual_schedule():
+            for it in range(-LC, NQ):
+                last = it == NQ - 1
+                if ok(it + LC):
+                    cast(it + LC)
+                if ok(it):
+                    group(it, 0, 4)
+                    mult(it, 0)
+                    mult(it, 1)
+                    mult(it, 2)
+                if ok(it + 1):
+                    quant(it + 1)
+                    mx(it + 1, 0)
+                    mx(it + 1, 1)
+                    mx(it + 1, 2)
+                if ok(it + 2):
+                    new_xg(it + 2)
+                    inter(it + 2)
+                    inter_s(it + 2)
+                if ok(it):
+                    mult(it, 3)
+                if ok(it + 1):
+                    mx(it + 1, 3)
+                if ok(it):
+                    add_store(it, 0, 4, nc.vector if last else nc.gpsimd)
+                if ok(it + 3):
+                    trans(it + 3)
+                    leave_s(it + 3)
+                if ok(it + 2):
+                    leave_v(it + 2)

@@ -19,11 +19,10 @@ P = 128
 TPP = S // P
 QPB = TPP // 4
 NQ = B * QPB
-PATH = "VUUUUUUUUUUUUUUU"
 LC = 4
-RVB = 48
 RG = 64
-RP = 256 - RVB
+SHARE = ((256, 256), (256, 256), (256, 0), (256, 0), (256, 0), (256, 0), (256, 0), (256, 0), (256, 0), (256, 0), (256, 0), (256, 0), (256, 0), (256, 0), (256, 0), (0, 0))
+assert len(SHARE) == NQ
 FLOPS = 2 * B * S * D * 256
 
 
@@ -101,23 +100,29 @@ def tile_attention_pa_t_kernel(tc, x_bytes, x_scale, Wq, Wk, rope_cos, rope_sin,
                 st[("xt", q, a)] = xt
 
         def leave_s(q):
-            if PATH[q] == "U":
-                xt = st[("xt", q, 1)]
-                pl = work.tile([P, 4, RP], BF16, name="pl")
-                st[("pl", q)] = pl
-                for u in range(2):
-                    for e in range(2):
-                        nc.scalar.activation(out=pl[:, 2 * u + e, :], in_=xt[:].bitcast(BF16)[:, u, 2 * RVB + e:512:2], func=COPY, scale=s4[:, u, e:e + 1])
+            for a in range(2):
+                n = SHARE[q][a]
+                if n < 256:
+                    xt = st[("xt", q, a)]
+                    pl = work.tile([P, 4, 256 - n], BF16, name="pl%d" % a)
+                    st[("pl", q, a)] = pl
+                    for u in range(2):
+                        for e in range(2):
+                            nc.scalar.activation(out=pl[:, 2 * u + e, :], in_=xt[:].bitcast(BF16)[:, u, 2 * n + e:512:2], func=COPY, scale=s4[:, u, e:e + 1])
 
         def new_xg(q):
             xg = xgp.tile([P, 4 * D], BF16, name="xg", align_bytes=64)
             st[("xg", q)] = xg
 
+        def g_cols(q):
+            return min(RG, 256 - SHARE[q][1])
+
         def inter(q):
-            if PATH[q] == "U":
+            n, g = SHARE[q][1], g_cols(q)
+            if g > 0:
                 nc.gpsimd.tensor_scalar(
-                    out=st[("xg", q)][:, 2 * D + 4 * RVB:2 * D + 4 * (RVB + RG)].rearrange("p (r t) -> p r t", t=4),
-                    in0=st[("pl", q)][:, :, 0:RG].rearrange("p t r -> p r t"),
+                    out=st[("xg", q)][:, 2 * D + 4 * n:2 * D + 4 * (n + g)].rearrange("p (r t) -> p r t", t=4),
+                    in0=st[("pl", q, 1)][:, :, 0:g].rearrange("p t r -> p r t"),
                     scalar1=1.0,
                     scalar2=0.0,
                     op0=MULT,
@@ -125,22 +130,27 @@ def tile_attention_pa_t_kernel(tc, x_bytes, x_scale, Wq, Wk, rope_cos, rope_sin,
                 )
 
         def inter_s(q):
-            if PATH[q] == "U":
-                nc.scalar.copy(
-                    out=st[("xg", q)][:, 2 * D + 4 * (RVB + RG):4 * D].rearrange("p (r t) -> p r t", t=4),
-                    in_=st[("pl", q)][:, :, RG:RP].rearrange("p t r -> p r t"),
-                )
+            for a in (0, 1):
+                n = SHARE[q][a]
+                g = g_cols(q) if a == 1 else 0
+                if n + g < 256:
+                    nc.scalar.copy(
+                        out=st[("xg", q)][:, a * 2 * D + 4 * (n + g):(a + 1) * 2 * D].rearrange("p (r t) -> p r t", t=4),
+                        in_=st[("pl", q, a)][:, :, g:256 - n].rearrange("p t r -> p r t"),
+                    )
 
         def leave_v(q):
             xg = st[("xg", q)]
-            for a, n in ((0, 256), (1, 256 if PATH[q] == "V" else RVB)):
-                xt = st[("xt", q, a)]
-                nc.vector.tensor_tensor(
-                    out=xg[:, a * 1024:a * 1024 + 4 * n].rearrange("p (r u e) -> p r u e", u=2, e=2),
-                    in0=xt[:].bitcast(BF16)[:, :, 0:2 * n].rearrange("p u (r e) -> p r u e", e=2),
-                    in1=s4[:].unsqueeze(1).to_broadcast([P, n, 2, 2]),
-                    op=MULT,
-                )
+            for a in range(2):
+                n = SHARE[q][a]
+                if n > 0:
+                    xt = st[("xt", q, a)]
+                    nc.vector.tensor_tensor(
+                        out=xg[:, a * 1024:a * 1024 + 4 * n].rearrange("p (r u e) -> p r u e", u=2, e=2),
+                        in0=xt[:].bitcast(BF16)[:, :, 0:2 * n].rearrange("p u (r e) -> p r u e", e=2),
+                        in1=s4[:].unsqueeze(1).to_broadcast([P, n, 2, 2]),
+                        op=MULT,
+                    )
 
         def quant(q):
             xc = work.tile([P, 4 * P], U32, name="xc", align_bytes=64)
@@ -196,6 +206,8 @@ def tile_attention_pa_t_kernel(tc, x_bytes, x_scale, Wq, Wk, rope_cos, rope_sin,
                 last = it == NQ - 1
                 if ok(it + LC):
                     cast(it + LC)
+                if ok(it + 3):
+                    trans(it + 3)
                 if ok(it):
                     group(it, 0, 4)
                     mult(it, 0)
@@ -217,7 +229,6 @@ def tile_attention_pa_t_kernel(tc, x_bytes, x_scale, Wq, Wk, rope_cos, rope_sin,
                 if ok(it):
                     add_store(it, 0, 4, nc.vector if last else nc.gpsimd)
                 if ok(it + 3):
-                    trans(it + 3)
                     leave_s(it + 3)
                 if ok(it + 2):
                     leave_v(it + 2)

@@ -121,8 +121,8 @@ def tile_attention_pa_t_kernel(tc, x_bytes, x_scale, Wq, Wk, rope_cos, rope_sin,
             n, g = SHARE[q][1], g_cols(q)
             if g > 0:
                 nc.gpsimd.tensor_scalar(
-                    out=st[("xg", q)][:, 2 * D + 4 * n:2 * D + 4 * (n + g)].rearrange("p (r t) -> p r t", t=4),
-                    in0=st[("pl", q, 1)][:, :, 0:g].rearrange("p t r -> p r t"),
+                    out=st[("xg", q)][:, 2 * D + 4 * n:2 * D + 4 * (n + g)].rearrange("p (c i t) -> p c t i", i=4, t=4),
+                    in0=st[("pl", q, 1)][:, :, 0:g].rearrange("p t (c i) -> p c t i", i=4),
                     scalar1=1.0,
                     scalar2=0.0,
                     op0=MULT,
@@ -135,8 +135,8 @@ def tile_attention_pa_t_kernel(tc, x_bytes, x_scale, Wq, Wk, rope_cos, rope_sin,
                 g = g_cols(q) if a == 1 else 0
                 if n + g < 256:
                     nc.scalar.copy(
-                        out=st[("xg", q)][:, a * 2 * D + 4 * (n + g):(a + 1) * 2 * D].rearrange("p (r t) -> p r t", t=4),
-                        in_=st[("pl", q, a)][:, :, g:256 - n].rearrange("p t r -> p r t"),
+                        out=st[("xg", q)][:, a * 2 * D + 4 * (n + g):(a + 1) * 2 * D].rearrange("p (c i t) -> p c t i", i=4, t=4),
+                        in_=st[("pl", q, a)][:, :, g:256 - n].rearrange("p t (c i) -> p c t i", i=4),
                     )
 
         def leave_v(q):

@@ -51,14 +51,16 @@ def tile_attention_pa_t_kernel(tc, x_bytes, x_scale, Wq, Wk, rope_cos, rope_sin,
         load(0)
         load(1)
         w_raw = keep.tile([P, 2, D], BF16, name="w_raw")
-        nc.scalar.dma_start(out=w_raw[:, 0, :], in_=Wq)
-        nc.scalar.dma_start(out=w_raw[:, 1, :], in_=Wk)
+        nc.sync.dma_start(out=w_raw[:, 0, :], in_=Wq)
+        nc.sync.dma_start(out=w_raw[:, 1, :], in_=Wk)
         s4 = keep.tile([P, 2, 2], F32, name="s4")
-        nc.scalar.dma_start(out=s4[:].rearrange("p u e -> p (u e)"), in_=x_scale.rearrange("a b (p t) -> p (a b t)", t=4))
+        nc.sync.dma_start(out=s4[:].rearrange("p u e -> p (u e)"), in_=x_scale.rearrange("a b (p t) -> p (a b t)", t=4))
+        load(2)
+        load(3)
         tab = keep.tile([P, TPP, 2, 64], BF16, name="tab")
-        nc.scalar.dma_start(out=tab[:, :, 0, :], in_=rope_cos.rearrange("(p i) f -> p i f", i=TPP))
-        nc.scalar.dma_start(out=tab[:, :, 1, :], in_=rope_sin.rearrange("(p i) f -> p i f", i=TPP))
-        for j in range(2, 2 * NQ):
+        nc.sync.dma_start(out=tab[:, :, 0, :], in_=rope_cos.rearrange("(p i) f -> p i f", i=TPP))
+        nc.sync.dma_start(out=tab[:, :, 1, :], in_=rope_sin.rearrange("(p i) f -> p i f", i=TPP))
+        for j in range(4, 2 * NQ):
             load(j)
 
         ident = keep.tile([P, P], F32, name="ident")

@@ -21,8 +21,10 @@ QPB = TPP // 4
 NQ = B * QPB
 LC = 4
 RG = 64
-SHARE = ((256, 256), (256, 256), (256, 0), (256, 0), (256, 0), (256, 0), (256, 0), (256, 0), (256, 0), (256, 0), (256, 0), (256, 0), (256, 0), (256, 0), (256, 0), (0, 0))
+VCAST = (1, 3)
+SHARE = ((256, 256), (256, 256)) + ((256, 0),) * 13 + ((0, 0),)
 assert len(SHARE) == NQ
+LOADS = (0, 1, "scale", 2, 3, "wq", "wk", 4, 5, "sin", "cos")
 FLOPS = 2 * B * S * D * 256
 
 
@@ -42,26 +44,31 @@ def tile_attention_pa_t_kernel(tc, x_bytes, x_scale, Wq, Wk, rope_cos, rope_sin,
         for j in range(2 * NQ):
             t = xin.tile([P, 2 * D], U8, name="xbytes", tag="xbytes")
             xb.append(t)
-
-        def load(j):
-            b, pj = divmod(j, 2 * QPB)
-            src = x_bytes[b].rearrange("(p i) k -> p (i k)", i=TPP)
-            nc.sync.dma_start(out=xb[j][:], in_=src[:, pj * 2 * D:(pj + 1) * 2 * D])
-
-        load(0)
-        load(1)
         w_raw = keep.tile([P, 2, D], BF16, name="w_raw")
-        nc.sync.dma_start(out=w_raw[:, 0, :], in_=Wq)
-        nc.sync.dma_start(out=w_raw[:, 1, :], in_=Wk)
         s4 = keep.tile([P, 2, 2], F32, name="s4")
-        nc.sync.dma_start(out=s4[:].rearrange("p u e -> p (u e)"), in_=x_scale.rearrange("a b (p t) -> p (a b t)", t=4))
-        load(2)
-        load(3)
         tab = keep.tile([P, TPP, 2, 64], BF16, name="tab")
-        nc.sync.dma_start(out=tab[:, :, 0, :], in_=rope_cos.rearrange("(p i) f -> p i f", i=TPP))
-        nc.sync.dma_start(out=tab[:, :, 1, :], in_=rope_sin.rearrange("(p i) f -> p i f", i=TPP))
-        for j in range(4, 2 * NQ):
-            load(j)
+
+        def load(what):
+            if what == "wq":
+                nc.sync.dma_start(out=w_raw[:, 0, :], in_=Wq)
+            elif what == "wk":
+                nc.sync.dma_start(out=w_raw[:, 1, :], in_=Wk)
+            elif what == "scale":
+                nc.sync.dma_start(out=s4[:].rearrange("p u e -> p (u e)"), in_=x_scale.rearrange("a b (p t) -> p (a b t)", t=4))
+            elif what == "cos":
+                nc.sync.dma_start(out=tab[:, :, 0, :], in_=rope_cos.rearrange("(p i) f -> p i f", i=TPP))
+            elif what == "sin":
+                nc.sync.dma_start(out=tab[:, :, 1, :], in_=rope_sin.rearrange("(p i) f -> p i f", i=TPP))
+            else:
+                b, pj = divmod(what, 2 * QPB)
+                src = x_bytes[b].rearrange("(p i) k -> p (i k)", i=TPP)
+                nc.sync.dma_start(out=xb[what][:], in_=src[:, pj * 2 * D:(pj + 1) * 2 * D])
+
+        for what in LOADS:
+            load(what)
+        for j in range(2 * NQ):
+            if j not in LOADS:
+                load(j)
 
         ident = keep.tile([P, P], F32, name="ident")
         make_identity(nc, ident[:])
@@ -71,25 +78,34 @@ def tile_attention_pa_t_kernel(tc, x_bytes, x_scale, Wq, Wk, rope_cos, rope_sin,
         ws = keep.tile([P, 512], U8, name="ws", align_bytes=64)
         wg = keep.tile([P, 1024], BF16, name="wg", align_bytes=64)
         nc.vector.memset(ws[:].bitcast(I32), 0)
-        wt = ps_t.tile([P, 2, 256], F32, name="xt", tag="xt")
-        for qk in range(2):
-            words = w_raw[:, qk, :].bitcast(F32)
-            for u in range(2):
-                nc.tensor.transpose(wt[:, u, qk * P:(qk + 1) * P], words[:, u:256:2], ident[:])
-        nc.vector.tensor_copy(out=wg[:].bitcast(F32).rearrange("p (n u) -> p n u", u=2), in_=wt[:].rearrange("p u n -> p n u"))
-        nc.vector.quantize_mx(out=wc[:, 0:256].bitcast(FP8X4), scales=ws[:, 0:256], in_=wg[:])
-        wcv = wc[:].bitcast(I32).rearrange("p (c g h j) -> p c g h j", c=2, g=4, h=2)
-        wsv = ws[:].rearrange("p (c g h j) -> p c g h j", c=2, g=4, h=2)
-        for h in range(2):
-            nc.vector.tensor_copy(out=wcv[:, 1, :, h, :], in_=wcv[:, 0, :, 1 - h, :])
-            nc.vector.tensor_copy(out=wsv[:, 1, :, h, :], in_=wsv[:, 0, :, 1 - h, :])
 
         st = {}
 
+        def w_trans():
+            wt = ps_t.tile([P, 2, 256], F32, name="xt", tag="xt")
+            for qk in range(2):
+                words = w_raw[:, qk, :].bitcast(F32)
+                for u in range(2):
+                    nc.tensor.transpose(wt[:, u, qk * P:(qk + 1) * P], words[:, u:256:2], ident[:])
+            st["wt"] = wt
+
+        def w_quant():
+            nc.vector.tensor_copy(out=wg[:].bitcast(F32).rearrange("p (n u) -> p n u", u=2), in_=st["wt"][:].rearrange("p u n -> p n u"))
+            nc.vector.quantize_mx(out=wc[:, 0:256].bitcast(FP8X4), scales=ws[:, 0:256], in_=wg[:])
+            wcv = wc[:].bitcast(I32).rearrange("p (c g h j) -> p c g h j", c=2, g=4, h=2)
+            wsv = ws[:].rearrange("p (c g h j) -> p c g h j", c=2, g=4, h=2)
+            for h in range(2):
+                nc.gpsimd.tensor_copy(out=wcv[:, 1, :, h, :], in_=wcv[:, 0, :, 1 - h, :])
+                nc.gpsimd.tensor_copy(out=wsv[:, 1, :, h, :], in_=wsv[:, 0, :, 1 - h, :])
+
         def cast(q):
             for a in range(2):
+                j = 2 * q + a
                 vb = deep.tile([P, 2 * D], BF16, name="vb")
-                nc.scalar.copy(out=vb[:], in_=xb[2 * q + a][:].bitcast(FP8))
+                if j in VCAST:
+                    nc.vector.tensor_copy(out=vb[:], in_=xb[j][:].bitcast(FP8))
+                else:
+                    nc.scalar.copy(out=vb[:], in_=xb[j][:].bitcast(FP8))
                 st[("vb", q, a)] = vb
 
         def trans(q):
@@ -210,6 +226,8 @@ def tile_attention_pa_t_kernel(tc, x_bytes, x_scale, Wq, Wk, rope_cos, rope_sin,
                     cast(it + LC)
                 if ok(it + 3):
                     trans(it + 3)
+                if it + 3 == 0:
+                    w_trans()
                 if ok(it):
                     group(it, 0, 4)
                     mult(it, 0)
@@ -234,3 +252,5 @@ def tile_attention_pa_t_kernel(tc, x_bytes, x_scale, Wq, Wk, rope_cos, rope_sin,
                     leave_s(it + 3)
                 if ok(it + 2):
                     leave_v(it + 2)
+                if it + 2 == 0:
+                    w_quant()

@@ -20,7 +20,7 @@ TPP = S // P
 QPB = TPP // 4
 NQ = B * QPB
 LC = 4
-RG = 64
+RG = 0
 VCAST = (1, 3)
 SHARE = ((256, 256), (256, 256)) + ((256, 0),) * 13 + ((0, 0),)
 assert len(SHARE) == NQ

@@ -34,7 +34,7 @@ def tile_attention_pa_t_kernel(tc, x_bytes, x_scale, Wq, Wk, rope_cos, rope_sin,
         keep = ctx.enter_context(tc.tile_pool(name="keep", bufs=1))
         xin = ctx.enter_context(tc.tile_pool(name="xin", bufs=2 * NQ))
         deep = ctx.enter_context(tc.tile_pool(name="deep", bufs=2 * LC + 2))
-        xgp = ctx.enter_context(tc.tile_pool(name="xgp", bufs=1))
+        xgp = ctx.enter_context(tc.tile_pool(name="xgp", bufs=2))
         work = ctx.enter_context(tc.tile_pool(name="work", bufs=3))
         outp = ctx.enter_context(tc.tile_pool(name="outp", bufs=4))
         ps_t = ctx.enter_context(tc.psum_pool(name="ps_t", bufs=4))

@@ -74,39 +74,46 @@ def tile_attention_pa_t_kernel(tc, x_bytes, x_scale, Wq, Wk, rope_cos, rope_sin,
         make_identity(nc, ident[:])
         nc.gpsimd.tensor_scalar(out=tab[:, :, 1, 0:32], in0=tab[:, :, 1, 0:32], scalar1=-1.0, scalar2=0.0, op0=MULT, op1=ADD)
 
+        swap = keep.tile([P, P], F32, name="swap")
+        for h in range(2):
+            nc.vector.tensor_copy(
+                out=swap[:].rearrange("p (g h j) -> p g h j", g=2, h=2)[:, :, h, :],
+                in_=ident[:].rearrange("p (g h j) -> p g h j", g=2, h=2)[:, :, 1 - h, :],
+            )
+
         wc = keep.tile([P, 512], U32, name="wc", align_bytes=64)
         ws = keep.tile([P, 512], U8, name="ws", align_bytes=64)
-        wg = keep.tile([P, 1024], BF16, name="wg", align_bytes=64)
-        nc.vector.memset(ws[:].bitcast(I32), 0)
+        wg = keep.tile([P, 2048], BF16, name="wg", align_bytes=64)
 
         st = {}
 
         def w_trans():
-            wt = ps_t.tile([P, 2, 256], F32, name="xt", tag="xt")
-            for qk in range(2):
-                words = w_raw[:, qk, :].bitcast(F32)
-                for u in range(2):
-                    nc.tensor.transpose(wt[:, u, qk * P:(qk + 1) * P], words[:, u:256:2], ident[:])
-            st["wt"] = wt
+            for c, perm in enumerate((ident, swap)):
+                wt = ps_y.tile([P, 2, 256], F32, name="y")
+                for qk in range(2):
+                    words = w_raw[:, qk, :].bitcast(F32)
+                    for u in range(2):
+                        nc.tensor.transpose(wt[:, u, qk * P:(qk + 1) * P], words[:, u:256:2], perm[:])
+                st[("wt", c)] = wt
+
+        def w_copy():
+            for c in range(2):
+                nc.scalar.copy(
+                    out=wg[:, c * 1024:(c + 1) * 1024].bitcast(F32).rearrange("p (n u) -> p n u", u=2),
+                    in_=st[("wt", c)][:].rearrange("p u n -> p n u"),
+                )
 
         def w_quant():
-            nc.vector.tensor_copy(out=wg[:].bitcast(F32).rearrange("p (n u) -> p n u", u=2), in_=st["wt"][:].rearrange("p u n -> p n u"))
-            nc.vector.quantize_mx(out=wc[:, 0:256].bitcast(FP8X4), scales=ws[:, 0:256], in_=wg[:])
-            wcv = wc[:].bitcast(I32).rearrange("p (c g h j) -> p c g h j", c=2, g=4, h=2)
-            wsv = ws[:].rearrange("p (c g h j) -> p c g h j", c=2, g=4, h=2)
-            for h in range(2):
-                nc.gpsimd.tensor_copy(out=wcv[:, 1, :, h, :], in_=wcv[:, 0, :, 1 - h, :])
-                nc.gpsimd.tensor_copy(out=wsv[:, 1, :, h, :], in_=wsv[:, 0, :, 1 - h, :])
+            nc.vector.quantize_mx(out=wc[:].bitcast(FP8X4), scales=ws[:], in_=wg[:])
 
-        def cast(q):
-            for a in range(2):
-                j = 2 * q + a
-                vb = deep.tile([P, 2 * D], BF16, name="vb")
-                if j in VCAST:
-                    nc.vector.tensor_copy(out=vb[:], in_=xb[j][:].bitcast(FP8))
-                else:
-                    nc.scalar.copy(out=vb[:], in_=xb[j][:].bitcast(FP8))
-                st[("vb", q, a)] = vb
+        def cast1(q, a):
+            j = 2 * q + a
+            vb = deep.tile([P, 2 * D], BF16, name="vb")
+            if j in VCAST:
+                nc.vector.tensor_copy(out=vb[:], in_=xb[j][:].bitcast(FP8))
+            else:
+                nc.scalar.copy(out=vb[:], in_=xb[j][:].bitcast(FP8))
+            st[("vb", q, a)] = vb
 
         def trans(q):
             for a in range(2):
@@ -223,7 +230,10 @@ def tile_attention_pa_t_kernel(tc, x_bytes, x_scale, Wq, Wk, rope_cos, rope_sin,
             for it in range(-LC, NQ):
                 last = it == NQ - 1
                 if ok(it + LC):
-                    cast(it + LC)
+                    cast1(it + LC, 0)
+                    if it + 2 == 0:
+                        w_copy()
+                    cast1(it + LC, 1)
                 if ok(it + 3):
                     trans(it + 3)
                 if it + 3 == 0:
@@ -235,6 +245,8 @@ def tile_attention_pa_t_kernel(tc, x_bytes, x_scale, Wq, Wk, rope_cos, rope_sin,
                     mult(it, 2)
                 if ok(it + 1):
                     quant(it + 1)
+                    if it + 1 == 0:
+                        w_quant()
                     mx(it + 1, 0)
                     mx(it + 1, 1)
                     mx(it + 1, 2)
@@ -252,5 +264,3 @@ def tile_attention_pa_t_kernel(tc, x_bytes, x_scale, Wq, Wk, rope_cos, rope_sin,
                     leave_s(it + 3)
                 if ok(it + 2):
                     leave_v(it + 2)
-                if it + 2 == 0:
-                    w_quant()

@@ -243,14 +243,20 @@ def tile_attention_pa_t_kernel(tc, x_bytes, x_scale, Wq, Wk, rope_cos, rope_sin,
                     mult(it, 0)
                     mult(it, 1)
                     mult(it, 2)
+                if it + 2 == NQ - 1:
+                    new_xg(it + 2)
+                    inter_s(it + 2)
                 if ok(it + 1):
-                    quant(it + 1)
+                    if it + 1 < NQ - 1:
+                        quant(it + 1)
+                    if it + 2 == NQ - 1:
+                        quant(it + 2)
                     if it + 1 == 0:
                         w_quant()
                     mx(it + 1, 0)
                     mx(it + 1, 1)
                     mx(it + 1, 2)
-                if ok(it + 2):
+                if ok(it + 2) and it + 2 < NQ - 1:
                     new_xg(it + 2)
                     inter(it + 2)
                     inter_s(it + 2)

@@ -22,7 +22,7 @@ NQ = B * QPB
 LC = 4
 RG = 0
 VCAST = (1, 3)
-SHARE = ((256, 256), (256, 256)) + ((256, 0),) * 13 + ((0, 0),)
+SHARE = ((256, 256), (256, 128)) + ((256, 0),) * 13 + ((0, 0),)
 assert len(SHARE) == NQ
 LOADS = (0, 1, "scale", 2, 3, "wq", "wk", 4, 5, "sin", "cos")
 FLOPS = 2 * B * S * D * 256

from contextlib import ExitStack

import concourse.mybir as mybir
from concourse.masks import make_identity

F32 = mybir.dt.float32
BF16 = mybir.dt.bfloat16
U32 = mybir.dt.uint32
I32 = mybir.dt.int32
U8 = mybir.dt.uint8
FP8 = mybir.dt.float8_e4m3fn
FP8X4 = mybir.dt.float8_e4m3fn_x4
MULT = mybir.AluOpType.mult
ADD = mybir.AluOpType.add
COPY = mybir.ActivationFunctionType.Copy

B, S, D = 4, 2048, 512
P = 128
TPP = S // P
QPB = TPP // 4
NQ = B * QPB
LC = 4
RG = 0
VCAST = (1, 3)
SHARE = ((256, 256), (256, 128)) + ((256, 0),) * 13 + ((0, 0),)
assert len(SHARE) == NQ
LOADS = (0, 1, "scale", 2, 3, "wq", "wk", 4, 5, "sin", "cos")
FLOPS = 2 * B * S * D * 256


def tile_attention_pa_t_kernel(tc, x_bytes, x_scale, Wq, Wk, rope_cos, rope_sin, out_0, out_1):
    nc = tc.nc
    with ExitStack() as ctx:
        keep = ctx.enter_context(tc.tile_pool(name="keep", bufs=1))
        xin = ctx.enter_context(tc.tile_pool(name="xin", bufs=2 * NQ))
        deep = ctx.enter_context(tc.tile_pool(name="deep", bufs=2 * LC + 2))
        xgp = ctx.enter_context(tc.tile_pool(name="xgp", bufs=2))
        work = ctx.enter_context(tc.tile_pool(name="work", bufs=3))
        outp = ctx.enter_context(tc.tile_pool(name="outp", bufs=4))
        ps_t = ctx.enter_context(tc.psum_pool(name="ps_t", bufs=4))
        ps_y = ctx.enter_context(tc.psum_pool(name="ps_y", bufs=4))

        xb = []
        for j in range(2 * NQ):
            t = xin.tile([P, 2 * D], U8, name="xbytes", tag="xbytes")
            xb.append(t)
        w_raw = keep.tile([P, 2, D], BF16, name="w_raw")
        s4 = keep.tile([P, 2, 2], F32, name="s4")
        tab = keep.tile([P, TPP, 2, 64], BF16, name="tab")

        def load(what):
            if what == "wq":
                nc.sync.dma_start(out=w_raw[:, 0, :], in_=Wq)
            elif what == "wk":
                nc.sync.dma_start(out=w_raw[:, 1, :], in_=Wk)
            elif what == "scale":
                nc.sync.dma_start(out=s4[:].rearrange("p u e -> p (u e)"), in_=x_scale.rearrange("a b (p t) -> p (a b t)", t=4))
            elif what == "cos":
                nc.sync.dma_start(out=tab[:, :, 0, :], in_=rope_cos.rearrange("(p i) f -> p i f", i=TPP))
            elif what == "sin":
                nc.sync.dma_start(out=tab[:, :, 1, :], in_=rope_sin.rearrange("(p i) f -> p i f", i=TPP))
            else:
                b, pj = divmod(what, 2 * QPB)
                src = x_bytes[b].rearrange("(p i) k -> p (i k)", i=TPP)
                nc.sync.dma_start(out=xb[what][:], in_=src[:, pj * 2 * D:(pj + 1) * 2 * D])

        for what in LOADS:
            load(what)
        for j in range(2 * NQ):
            if j not in LOADS:
                load(j)

        ident = keep.tile([P, P], F32, name="ident")
        make_identity(nc, ident[:])
        nc.gpsimd.tensor_scalar(out=tab[:, :, 1, 0:32], in0=tab[:, :, 1, 0:32], scalar1=-1.0, scalar2=0.0, op0=MULT, op1=ADD)

        swap = keep.tile([P, P], F32, name="swap")
        for h in range(2):
            nc.vector.tensor_copy(
                out=swap[:].rearrange("p (g h j) -> p g h j", g=2, h=2)[:, :, h, :],
                in_=ident[:].rearrange("p (g h j) -> p g h j", g=2, h=2)[:, :, 1 - h, :],
            )

        wc = keep.tile([P, 512], U32, name="wc", align_bytes=64)
        ws = keep.tile([P, 512], U8, name="ws", align_bytes=64)
        wg = keep.tile([P, 2048], BF16, name="wg", align_bytes=64)

        st = {}

        def w_trans():
            for c, perm in enumerate((ident, swap)):
                wt = ps_y.tile([P, 2, 256], F32, name="y")
                for qk in range(2):
                    words = w_raw[:, qk, :].bitcast(F32)
                    for u in range(2):
                        nc.tensor.transpose(wt[:, u, qk * P:(qk + 1) * P], words[:, u:256:2], perm[:])
                st[("wt", c)] = wt

        def w_copy():
            for c in range(2):
                nc.scalar.copy(
                    out=wg[:, c * 1024:(c + 1) * 1024].bitcast(F32).rearrange("p (n u) -> p n u", u=2),
                    in_=st[("wt", c)][:].rearrange("p u n -> p n u"),
                )

        def w_quant():
            nc.vector.quantize_mx(out=wc[:].bitcast(FP8X4), scales=ws[:], in_=wg[:])

        def cast1(q, a):
            j = 2 * q + a
            vb = deep.tile([P, 2 * D], BF16, name="vb")
            if j in VCAST:
                nc.vector.tensor_copy(out=vb[:], in_=xb[j][:].bitcast(FP8))
            else:
                nc.scalar.copy(out=vb[:], in_=xb[j][:].bitcast(FP8))
            st[("vb", q, a)] = vb

        def trans(q):
            for a in range(2):
                vw = st[("vb", q, a)][:].bitcast(F32)
                xt = ps_t.tile([P, 2, 256], F32, name="xt", tag="xt")
                for tl in range(2):
                    for u in range(2):
                        nc.tensor.transpose(xt[:, u, tl * P:(tl + 1) * P], vw[:, tl * 256 + u:(tl + 1) * 256:2], ident[:])
                st[("xt", q, a)] = xt

        def leave_s(q):
            for a in range(2):
                n = SHARE[q][a]
                if n < 256:
                    xt = st[("xt", q, a)]
                    pl = work.tile([P, 4, 256 - n], BF16, name="pl%d" % a)
                    st[("pl", q, a)] = pl
                    for u in range(2):
                        for e in range(2):
                            nc.scalar.activation(out=pl[:, 2 * u + e, :], in_=xt[:].bitcast(BF16)[:, u, 2 * n + e:512:2], func=COPY, scale=s4[:, u, e:e + 1])

        def new_xg(q):
            xg = xgp.tile([P, 4 * D], BF16, name="xg", align_bytes=64)
            st[("xg", q)] = xg

        def g_cols(q):
            return min(RG, 256 - SHARE[q][1])

        def inter(q):
            n, g = SHARE[q][1], g_cols(q)
            if g > 0:
                nc.gpsimd.tensor_scalar(
                    out=st[("xg", q)][:, 2 * D + 4 * n:2 * D + 4 * (n + g)].rearrange("p (c i t) -> p c t i", i=4, t=4),
                    in0=st[("pl", q, 1)][:, :, 0:g].rearrange("p t (c i) -> p c t i", i=4),
                    scalar1=1.0,
                    scalar2=0.0,
                    op0=MULT,
                    op1=ADD,
                )

        def inter_s(q):
            for a in (0, 1):
                n = SHARE[q][a]
                g = g_cols(q) if a == 1 else 0
                if n + g < 256:
                    nc.scalar.copy(
                        out=st[("xg", q)][:, a * 2 * D + 4 * (n + g):(a + 1) * 2 * D].rearrange("p (c i t) -> p c t i", i=4, t=4),
                        in_=st[("pl", q, a)][:, :, g:256 - n].rearrange("p t (c i) -> p c t i", i=4),
                    )

        def leave_v(q):
            xg = st[("xg", q)]
            for a in range(2):
                n = SHARE[q][a]
                if n > 0:
                    xt = st[("xt", q, a)]
                    nc.vector.tensor_tensor(
                        out=xg[:, a * 1024:a * 1024 + 4 * n].rearrange("p (r u e) -> p r u e", u=2, e=2),
                        in0=xt[:].bitcast(BF16)[:, :, 0:2 * n].rearrange("p u (r e) -> p r u e", e=2),
                        in1=s4[:].unsqueeze(1).to_broadcast([P, n, 2, 2]),
                        op=MULT,
                    )

        def quant(q):
            xc = work.tile([P, 4 * P], U32, name="xc", align_bytes=64)
            xs = work.tile([P, 4 * P], U8, name="xs", align_bytes=64)
            nc.vector.quantize_mx(out=xc[:].bitcast(FP8X4), scales=xs[:], in_=st[("xg", q)][:])
            st[("xc", q)] = xc
            st[("xs", q)] = xs

        def mx(q, tl):
            y = ps_y.tile([P, 512], F32, name="y")
            cols = slice(tl * P, (tl + 1) * P)
            nc.tensor.matmul_mx(
                out=y[:],
                lhsT=st[("xc", q)][:, cols].bitcast(FP8X4),
                lhsT_scale=st[("xs", q)][:, cols],
                rhs=wc[:].bitcast(FP8X4),
                rhs_scale=ws[:],
                start=True,
                stop=True,
            )
            st[("y", q, tl)] = y

        def group(q, t0, t1):
            prod = outp.tile([P, 2, 4, t1 - t0, 64], F32, name="prod")
            st[("prod", q)] = (prod, t0)

        def mult(q, tl):
            i = (q % QPB) * 4 + tl
            prod, t0 = st[("prod", q)]
            nc.vector.tensor_tensor(
                out=prod[:, :, :, tl - t0, :],
                in0=st[("y", q, tl)][:].rearrange("p (c g f) -> p c g f", c=2, g=4),
                in1=tab[:, i, :, :].unsqueeze(2).to_broadcast([P, 2, 4, 64]),
                op=MULT,
            )

        def add_store(q, t0, t1, eng):
            b, m = divmod(q, QPB)
            prod, t00 = st[("prod", q)]
            stage = outp.tile([P, 4, t1 - t0, 64], F32, name="stage")
            eng.tensor_tensor(out=stage[:], in0=prod[:, 0, :, :, :], in1=prod[:, 1, :, :, :], op=ADD)
            for o, dst in enumerate((out_0, out_1)):
                nc.sync.dma_start(
                    out=dst[b].rearrange("h (p i) f -> p h (i f)", i=TPP)[:, :, (m * 4 + t0) * 64:(m * 4 + t1) * 64],
                    in_=stage[:, 2 * o:2 * o + 2, :, :].rearrange("p g t f -> p g (t f)"),
                )

        def ok(q):
            return 0 <= q < NQ

        with tc.manual_schedule():
            for it in range(-LC, NQ):
                last = it == NQ - 1
                if ok(it + LC):
                    cast1(it + LC, 0)
                    if it + 2 == 0:
                        w_copy()
                    cast1(it + LC, 1)
                if ok(it + 3):
                    trans(it + 3)
                if it + 3 == 0:
                    w_trans()
                if ok(it):
                    group(it, 0, 4)
                    mult(it, 0)
                    mult(it, 1)
                    mult(it, 2)
                if it + 2 == NQ - 1:
                    new_xg(it + 2)
                    inter_s(it + 2)
                if ok(it + 1):
                    if it + 1 < NQ - 1:
                        quant(it + 1)
                    if it + 2 == NQ - 1:
                        quant(it + 2)
                    if it + 1 == 0:
                        w_quant()
                    mx(it + 1, 0)
                    mx(it + 1, 1)
                    mx(it + 1, 2)
                if ok(it + 2) and it + 2 < NQ - 1:
                    new_xg(it + 2)
                    inter(it + 2)
                    inter_s(it + 2)
                if ok(it):
                    mult(it, 3)
                if ok(it + 1):
                    mx(it + 1, 3)
                if ok(it):
                    add_store(it, 0, 4, nc.vector if last else nc.gpsimd)
                if ok(it + 3):
                    leave_s(it + 3)
                if ok(it + 2):
                    leave_v(it + 2)
